import numpy as np
import ml_dtypes


def mxq(x, axis, fmt="e4m3"):
    dtype, down = {"e4m3": (ml_dtypes.float8_e4m3fn, 7), "e5m2": (ml_dtypes.float8_e5m2, 14)}[fmt]
    v = np.moveaxis(np.asarray(x, np.float32).astype(ml_dtypes.bfloat16).astype(np.float64), axis, -1)
    blocks = v.reshape(v.shape[:-1] + (-1, 32))
    amax = np.abs(blocks).max(-1, keepdims=True)
    byte = np.maximum(np.where(amax > 0, np.frexp(amax)[1] - 1 + 127, 0) - down, 1)
    scale = np.exp2(byte - 127.0)
    codes = (blocks / scale).astype(np.float32).astype(dtype).astype(np.float64)
    return np.moveaxis((codes * scale).reshape(v.shape), -1, axis)


BF16 = ml_dtypes.bfloat16


def bf(x):
    return np.asarray(x, np.float32).astype(BF16)


def f64(x):
    return np.asarray(x).astype(np.float64)


N, D, P, G = 640, 512, 1, 16
EPS = 1e-12
EPSILON = 0.65


def setup_inputs():
    centres = np.random.standard_normal((G, D))
    which = np.random.randint(0, G, N)
    features = centres[which] + 0.4 * np.random.standard_normal((N, D))
    limit = np.sqrt(6.0 / (P + D))
    return {"features": bf(features), "weight_tensor": bf(np.random.uniform(-limit, limit, (P, D)))}


def reference(features, weight_tensor):
    features, weight_tensor = f64(features), f64(weight_tensor)
    context = features[None, :, :] * weight_tensor[:, None, :]
    norm = np.sqrt((context ** 2).sum(-1, keepdims=True))
    context_norm = context / np.maximum(norm, EPS)
    c = context_norm.transpose(1, 0, 2).reshape(N, P * D)
    cq = mxq(c, 1, "e4m3")
    similarity = (cq @ cq.T) / P
    adj = np.where(similarity > EPSILON, similarity, 0.0)
    return (adj + adj.T) * 0.5

@@ -1,0 +1,146 @@
+from contextlib import ExitStack
+
+import concourse.mybir as mybir
+from concourse.masks import make_identity
+
+F32 = mybir.dt.float32
+BF16 = mybir.dt.bfloat16
+U32 = mybir.dt.uint32
+U8 = mybir.dt.uint8
+FP8X4 = mybir.dt.float8_e4m3fn_x4
+ALU = mybir.AluOpType
+ACT = mybir.ActivationFunctionType
+
+P = 128
+PACK = 4
+N_ROWS = 640
+D = 512
+BLOCKS = N_ROWS // P
+WIDE_BLOCKS = 4
+WIDE = WIDE_BLOCKS * P
+EPS = 1e-12
+EPSILON = 0.65
+
+FLOPS = 2 * N_ROWS * N_ROWS * D
+
+
+def tile_graphlearner_s_kernel(tc, features, weight_tensor, out):
+    nc = tc.nc
+    with ExitStack() as ctx:
+        consts = ctx.enter_context(tc.tile_pool(name="consts", bufs=1))
+        keep = ctx.enter_context(tc.tile_pool(name="keep", bufs=1))
+        work = ctx.enter_context(tc.tile_pool(name="work", bufs=BLOCKS))
+        results = ctx.enter_context(tc.tile_pool(name="results", bufs=4))
+        psum_w = ctx.enter_context(tc.psum_pool(name="psum_w", bufs=1))
+        psum_t = ctx.enter_context(tc.psum_pool(name="psum_t", bufs=2))
+        psum_s = ctx.enter_context(tc.psum_pool(name="psum_s", bufs=5))
+
+        feat = keep.tile([P, BLOCKS, D], BF16)
+        for b in range(BLOCKS):
+            nc.sync.dma_start(out=feat[:, b, :], in_=features[b * P : (b + 1) * P, :])
+        w_row = consts.tile([P, D], BF16)
+        nc.vector.memset(w_row[:], 0.0)
+        nc.scalar.dma_start(out=w_row[0:1, :], in_=weight_tensor)
+
+        ones = consts.tile([P, P], BF16)
+        nc.vector.memset(ones[:], 1.0)
+        one_col = consts.tile([P, 1], F32)
+        nc.vector.memset(one_col[:], 1.0)
+        ident = consts.tile([P, P], BF16)
+        make_identity(nc, ident[:])
+        table_warm = consts.tile([P, 1], F32)
+        nc.scalar.activation(out=table_warm[:], in_=one_col[:], func=ACT.Abs_reciprocal_sqrt)
+
+        w_all = psum_w.tile([P, D], F32)
+        nc.tensor.matmul(out=w_all[:], lhsT=ones[:], rhs=w_row[:], start=True, stop=True)
+
+        sumsq = keep.tile([P, BLOCKS], F32)
+        rsqrt = keep.tile([P, BLOCKS], F32)
+        rnorm = keep.tile([P, BLOCKS], F32)
+        grouped = keep.tile([P, BLOCKS, P, PACK], BF16, align_bytes=64)
+        codes = keep.tile([P, N_ROWS], U32, align_bytes=64)
+        scales = keep.tile([P, N_ROWS], U8, align_bytes=64)
+        context = {}
+
+        def weigh(b):
+            ctx_b = work.tile([P, D], F32, name="ctx_b")
+            nc.vector.tensor_tensor(out=ctx_b[:], in0=feat[:, b, :], in1=w_all[:], op=ALU.mult)
+            squares = work.tile([P, D], BF16, name="squares")
+            nc.scalar.activation(
+                out=squares[:], in_=ctx_b[:], func=ACT.Square, accum_out=sumsq[:, b : b + 1]
+            )
+            context[b] = ctx_b
+
+        def quantise(b):
+            col = slice(b, b + 1)
+            rows = slice(b * P, (b + 1) * P)
+            nc.scalar.activation(out=rsqrt[:, col], in_=sumsq[:, col], func=ACT.Abs_reciprocal_sqrt)
+            nc.vector.tensor_scalar_min(out=rnorm[:, col], in0=rsqrt[:, col], scalar1=1.0 / EPS)
+            c_b = work.tile([P, D], BF16, name="c_b")
+            nc.vector.tensor_scalar_mul(out=c_b[:], in0=context[b][:], scalar1=rnorm[:, col])
+            c_t = psum_t.tile([P, PACK, P], BF16, name="c_t")
+            for t in range(PACK):
+                nc.tensor.transpose(c_t[:, t, :], c_b[:, t * P : (t + 1) * P], ident[:])
+            nc.scalar.copy(out=grouped[:, b], in_=c_t[:].rearrange("p t r -> p r t"))
+            nc.vector.quantize_mx(
+                out=codes[:, rows].bitcast(FP8X4),
+                scales=scales[:, rows],
+                in_=grouped[:, b].rearrange("p r t -> p (r t)"),
+            )
+
+        def similarity(acc, i, cols):
+            rows = slice(i * P, (i + 1) * P)
+            nc.tensor.matmul_mx(
+                out=acc,
+                lhsT=codes[:, rows].bitcast(FP8X4),
+                lhsT_scale=scales[:, rows],
+                rhs=codes[:, cols].bitcast(FP8X4),
+                rhs_scale=scales[:, cols],
+                start=True,
+                stop=True,
+            )
+
+        def threshold(acc, width):
+            sim = results.tile([P, WIDE], F32, name="sim")
+            nc.scalar.copy(out=sim[:, :width], in_=acc)
+            adj = results.tile([P, WIDE], F32, name="adj")
+            nc.vector.scalar_tensor_tensor(
+                out=adj[:, :width],
+                in0=sim[:, :width],
+                scalar=EPSILON,
+                in1=sim[:, :width],
+                op0=ALU.is_gt,
+                op1=ALU.mult,
+            )
+            return adj
+
+        def wide_part(i):
+            acc = psum_s.tile([P, WIDE], F32, name="acc")
+            similarity(acc[:], i, slice(0, WIDE))
+            adj = threshold(acc[:], WIDE)
+            nc.sync.dma_start(out=out[i * P : (i + 1) * P, 0:WIDE], in_=adj[:])
+
+        for b in range(BLOCKS):
+            weigh(b)
+        for b in range(WIDE_BLOCKS):
+            quantise(b)
+        for i in range(WIDE_BLOCKS):
+            wide_part(i)
+        for b in range(WIDE_BLOCKS, BLOCKS):
+            quantise(b)
+        for i in range(WIDE_BLOCKS, BLOCKS):
+            wide_part(i)
+
+        last_cols = slice(WIDE, N_ROWS)
+        acc = psum_s.tile([P, WIDE], F32, name="acc")
+        for i in range(WIDE_BLOCKS):
+            similarity(acc[:, i * P : (i + 1) * P], i, last_cols)
+        adj = threshold(acc[:], WIDE)
+        nc.sync.dma_start(
+            out=out[0:WIDE, last_cols].rearrange("(i p) m -> p i m", p=P),
+            in_=adj[:].rearrange("p (i m) -> p i m", m=P),
+        )
+        acc = psum_s.tile([P, WIDE], F32, name="acc")
+        similarity(acc[:, 0:P], WIDE_BLOCKS, last_cols)
+        adj = threshold(acc[:, 0:P], P)
+        nc.sync.dma_start(out=out[WIDE:N_ROWS, last_cols], in_=adj[:, 0:P])

@@ -18,6 +18,7 @@ D = 512
 BLOCKS = N_ROWS // P
 WIDE_BLOCKS = 4
 WIDE = WIDE_BLOCKS * P
+LEAD = 3
 EPS = 1e-12
 EPSILON = 0.65
 
@@ -32,8 +33,9 @@ def tile_graphlearner_s_kernel(tc, features, weight_tensor, out):
         work = ctx.enter_context(tc.tile_pool(name="work", bufs=BLOCKS))
         results = ctx.enter_context(tc.tile_pool(name="results", bufs=4))
         psum_w = ctx.enter_context(tc.psum_pool(name="psum_w", bufs=1))
-        psum_t = ctx.enter_context(tc.psum_pool(name="psum_t", bufs=2))
-        psum_s = ctx.enter_context(tc.psum_pool(name="psum_s", bufs=5))
+        psum_t = ctx.enter_context(tc.psum_pool(name="psum_t", bufs=3))
+        psum_s = ctx.enter_context(tc.psum_pool(name="psum_s", bufs=4))
+        ctx.enter_context(tc.manual_schedule())
 
         feat = keep.tile([P, BLOCKS, D], BF16)
         for b in range(BLOCKS):
@@ -61,27 +63,36 @@ def tile_graphlearner_s_kernel(tc, features, weight_tensor, out):
         codes = keep.tile([P, N_ROWS], U32, align_bytes=64)
         scales = keep.tile([P, N_ROWS], U8, align_bytes=64)
         context = {}
+        transposed = {}
 
         def weigh(b):
+            col = slice(b, b + 1)
             ctx_b = work.tile([P, D], F32, name="ctx_b")
             nc.vector.tensor_tensor(out=ctx_b[:], in0=feat[:, b, :], in1=w_all[:], op=ALU.mult)
             squares = work.tile([P, D], BF16, name="squares")
-            nc.scalar.activation(
-                out=squares[:], in_=ctx_b[:], func=ACT.Square, accum_out=sumsq[:, b : b + 1]
-            )
+            nc.scalar.activation(out=squares[:], in_=ctx_b[:], func=ACT.Square, accum_out=sumsq[:, col])
+            nc.scalar.activation(out=rsqrt[:, col], in_=sumsq[:, col], func=ACT.Abs_reciprocal_sqrt)
             context[b] = ctx_b
 
-        def quantise(b):
+        def normalise(b):
             col = slice(b, b + 1)
-            rows = slice(b * P, (b + 1) * P)
-            nc.scalar.activation(out=rsqrt[:, col], in_=sumsq[:, col], func=ACT.Abs_reciprocal_sqrt)
             nc.vector.tensor_scalar_min(out=rnorm[:, col], in0=rsqrt[:, col], scalar1=1.0 / EPS)
             c_b = work.tile([P, D], BF16, name="c_b")
             nc.vector.tensor_scalar_mul(out=c_b[:], in0=context[b][:], scalar1=rnorm[:, col])
             c_t = psum_t.tile([P, PACK, P], BF16, name="c_t")
             for t in range(PACK):
                 nc.tensor.transpose(c_t[:, t, :], c_b[:, t * P : (t + 1) * P], ident[:])
-            nc.scalar.copy(out=grouped[:, b], in_=c_t[:].rearrange("p t r -> p r t"))
+            transposed[b] = c_t
+
+        def pack(b):
+            planes = transposed[b][:].rearrange("p t r -> p r t")
+            if b % 2 == 0:
+                nc.scalar.copy(out=grouped[:, b], in_=planes)
+            else:
+                nc.vector.tensor_copy(out=grouped[:, b], in_=planes)
+
+        def quantise(b):
+            rows = slice(b * P, (b + 1) * P)
             nc.vector.quantize_mx(
                 out=codes[:, rows].bitcast(FP8X4),
                 scales=scales[:, rows],
@@ -114,22 +125,23 @@ def tile_graphlearner_s_kernel(tc, features, weight_tensor, out):
             )
             return adj
 
-        def wide_part(i):
+        for b in range(LEAD):
+            weigh(b)
+        for step in range(BLOCKS + 2):
+            if step < BLOCKS:
+                normalise(step)
+            if 0 <= step - 1 < BLOCKS:
+                pack(step - 1)
+            if step + LEAD < BLOCKS:
+                weigh(step + LEAD)
+            if 0 <= step - 2 < BLOCKS:
+                quantise(step - 2)
+
+        for i in range(BLOCKS):
             acc = psum_s.tile([P, WIDE], F32, name="acc")
             similarity(acc[:], i, slice(0, WIDE))
             adj = threshold(acc[:], WIDE)
             nc.sync.dma_start(out=out[i * P : (i + 1) * P, 0:WIDE], in_=adj[:])
-
-        for b in range(BLOCKS):
-            weigh(b)
-        for b in range(WIDE_BLOCKS):
-            quantise(b)
-        for i in range(WIDE_BLOCKS):
-            wide_part(i)
-        for b in range(WIDE_BLOCKS, BLOCKS):
-            quantise(b)
-        for i in range(WIDE_BLOCKS, BLOCKS):
-            wide_part(i)
 
         last_cols = slice(WIDE, N_ROWS)
         acc = psum_s.tile([P, WIDE], F32, name="acc")

@@ -31,7 +31,7 @@ def tile_graphlearner_s_kernel(tc, features, weight_tensor, out):
         consts = ctx.enter_context(tc.tile_pool(name="consts", bufs=1))
         keep = ctx.enter_context(tc.tile_pool(name="keep", bufs=1))
         work = ctx.enter_context(tc.tile_pool(name="work", bufs=BLOCKS))
-        results = ctx.enter_context(tc.tile_pool(name="results", bufs=4))
+        results = ctx.enter_context(tc.tile_pool(name="results", bufs=BLOCKS + 2))
         psum_w = ctx.enter_context(tc.psum_pool(name="psum_w", bufs=1))
         psum_t = ctx.enter_context(tc.psum_pool(name="psum_t", bufs=3))
         psum_s = ctx.enter_context(tc.psum_pool(name="psum_s", bufs=4))

@@ -40,21 +40,27 @@ def tile_graphlearner_s_kernel(tc, features, weight_tensor, out):
         feat = keep.tile([P, BLOCKS, D], BF16)
         for b in range(BLOCKS):
             nc.sync.dma_start(out=feat[:, b, :], in_=features[b * P : (b + 1) * P, :])
-        w_row = consts.tile([P, D], BF16)
-        nc.vector.memset(w_row[:], 0.0)
-        nc.scalar.dma_start(out=w_row[0:1, :], in_=weight_tensor)
+        w_cols = consts.tile([P, PACK], BF16)
+        nc.scalar.dma_start(out=w_cols[:], in_=weight_tensor.rearrange("o (p t) -> (o p) t", t=PACK))
 
-        ones = consts.tile([P, P], BF16)
-        nc.vector.memset(ones[:], 1.0)
         one_col = consts.tile([P, 1], F32)
         nc.vector.memset(one_col[:], 1.0)
         ident = consts.tile([P, P], BF16)
         make_identity(nc, ident[:])
+        ident_f32 = consts.tile([P, P], F32)
+        make_identity(nc, ident_f32[:])
         table_warm = consts.tile([P, 1], F32)
         nc.scalar.activation(out=table_warm[:], in_=one_col[:], func=ACT.Abs_reciprocal_sqrt)
 
-        w_all = psum_w.tile([P, D], F32)
-        nc.tensor.matmul(out=w_all[:], lhsT=ones[:], rhs=w_row[:], start=True, stop=True)
+        w_all = psum_w.tile([P, PACK, P], F32)
+        for t in range(PACK):
+            nc.tensor.matmul(
+                out=w_all[:, t, :],
+                lhsT=w_cols[:, t : t + 1].to_broadcast([P, P]),
+                rhs=ident[:],
+                start=True,
+                stop=True,
+            )
 
         sumsq = keep.tile([P, BLOCKS], F32)
         rsqrt = keep.tile([P, BLOCKS], F32)
@@ -68,7 +74,12 @@ def tile_graphlearner_s_kernel(tc, features, weight_tensor, out):
         def weigh(b):
             col = slice(b, b + 1)
             ctx_b = work.tile([P, D], F32, name="ctx_b")
-            nc.vector.tensor_tensor(out=ctx_b[:], in0=feat[:, b, :], in1=w_all[:], op=ALU.mult)
+            nc.vector.tensor_tensor(
+                out=ctx_b[:].rearrange("p (u n e) -> p u n e", u=2, e=2),
+                in0=feat[:, b, :].rearrange("p (n u e) -> p u n e", u=2, e=2),
+                in1=w_all[:].rearrange("p (u e) n -> p u n e", u=2),
+                op=ALU.mult,
+            )
             squares = work.tile([P, D], BF16, name="squares")
             nc.scalar.activation(out=squares[:], in_=ctx_b[:], func=ACT.Square, accum_out=sumsq[:, col])
             nc.scalar.activation(out=rsqrt[:, col], in_=sumsq[:, col], func=ACT.Abs_reciprocal_sqrt)
@@ -79,17 +90,18 @@ def tile_graphlearner_s_kernel(tc, features, weight_tensor, out):
             nc.vector.tensor_scalar_min(out=rnorm[:, col], in0=rsqrt[:, col], scalar1=1.0 / EPS)
             c_b = work.tile([P, D], BF16, name="c_b")
             nc.vector.tensor_scalar_mul(out=c_b[:], in0=context[b][:], scalar1=rnorm[:, col])
-            c_t = psum_t.tile([P, PACK, P], BF16, name="c_t")
-            for t in range(PACK):
-                nc.tensor.transpose(c_t[:, t, :], c_b[:, t * P : (t + 1) * P], ident[:])
+            words = c_b[:].bitcast(F32)
+            c_t = psum_t.tile([P, 2, P], F32, name="c_t")
+            for u in range(2):
+                nc.tensor.transpose(c_t[:, u, :], words[:, u * P : (u + 1) * P], ident_f32[:])
             transposed[b] = c_t
 
         def pack(b):
-            planes = transposed[b][:].rearrange("p t r -> p r t")
+            planes = transposed[b][:].rearrange("p u r -> p r u")
             if b % 2 == 0:
-                nc.scalar.copy(out=grouped[:, b], in_=planes)
+                nc.scalar.copy(out=grouped[:, b].bitcast(F32), in_=planes)
             else:
-                nc.vector.tensor_copy(out=grouped[:, b], in_=planes)
+                nc.vector.tensor_copy(out=grouped[:, b].bitcast(F32), in_=planes)
 
         def quantise(b):
             rows = slice(b * P, (b + 1) * P)

@@ -18,7 +18,6 @@ D = 512
 BLOCKS = N_ROWS // P
 WIDE_BLOCKS = 4
 WIDE = WIDE_BLOCKS * P
-LEAD = 3
 EPS = 1e-12
 EPSILON = 0.65
 
@@ -31,7 +30,7 @@ def tile_graphlearner_s_kernel(tc, features, weight_tensor, out):
         consts = ctx.enter_context(tc.tile_pool(name="consts", bufs=1))
         keep = ctx.enter_context(tc.tile_pool(name="keep", bufs=1))
         work = ctx.enter_context(tc.tile_pool(name="work", bufs=BLOCKS))
-        results = ctx.enter_context(tc.tile_pool(name="results", bufs=BLOCKS + 2))
+        results = ctx.enter_context(tc.tile_pool(name="results", bufs=2 * BLOCKS))
         psum_w = ctx.enter_context(tc.psum_pool(name="psum_w", bufs=1))
         psum_t = ctx.enter_context(tc.psum_pool(name="psum_t", bufs=3))
         psum_s = ctx.enter_context(tc.psum_pool(name="psum_s", bufs=4))
@@ -69,10 +68,10 @@ def tile_graphlearner_s_kernel(tc, features, weight_tensor, out):
         codes = keep.tile([P, N_ROWS], U32, align_bytes=64)
         scales = keep.tile([P, N_ROWS], U8, align_bytes=64)
         context = {}
+        normalised = {}
         transposed = {}
 
         def weigh(b):
-            col = slice(b, b + 1)
             ctx_b = work.tile([P, D], F32, name="ctx_b")
             nc.vector.tensor_tensor(
                 out=ctx_b[:].rearrange("p (u n e) -> p u n e", u=2, e=2),
@@ -80,28 +79,32 @@ def tile_graphlearner_s_kernel(tc, features, weight_tensor, out):
                 in1=w_all[:].rearrange("p (u e) n -> p u n e", u=2),
                 op=ALU.mult,
             )
-            squares = work.tile([P, D], BF16, name="squares")
-            nc.scalar.activation(out=squares[:], in_=ctx_b[:], func=ACT.Square, accum_out=sumsq[:, col])
-            nc.scalar.activation(out=rsqrt[:, col], in_=sumsq[:, col], func=ACT.Abs_reciprocal_sqrt)
             context[b] = ctx_b
+
+        def sum_squares(b):
+            squares = work.tile([P, D], BF16, name="squares")
+            nc.scalar.activation(out=squares[:], in_=context[b][:], func=ACT.Square, accum_out=sumsq[:, b : b + 1])
+
+        def root(b):
+            col = slice(b, b + 1)
+            nc.scalar.activation(out=rsqrt[:, col], in_=sumsq[:, col], func=ACT.Abs_reciprocal_sqrt)
 
         def normalise(b):
             col = slice(b, b + 1)
             nc.vector.tensor_scalar_min(out=rnorm[:, col], in0=rsqrt[:, col], scalar1=1.0 / EPS)
             c_b = work.tile([P, D], BF16, name="c_b")
             nc.vector.tensor_scalar_mul(out=c_b[:], in0=context[b][:], scalar1=rnorm[:, col])
-            words = c_b[:].bitcast(F32)
+            normalised[b] = c_b
+
+        def transpose(b):
+            words = normalised[b][:].bitcast(F32)
             c_t = psum_t.tile([P, 2, P], F32, name="c_t")
             for u in range(2):
                 nc.tensor.transpose(c_t[:, u, :], words[:, u * P : (u + 1) * P], ident_f32[:])
             transposed[b] = c_t
 
         def pack(b):
-            planes = transposed[b][:].rearrange("p u r -> p r u")
-            if b % 2 == 0:
-                nc.scalar.copy(out=grouped[:, b].bitcast(F32), in_=planes)
-            else:
-                nc.vector.tensor_copy(out=grouped[:, b].bitcast(F32), in_=planes)
+            nc.scalar.copy(out=grouped[:, b].bitcast(F32), in_=transposed[b][:].rearrange("p u r -> p r u"))
 
         def quantise(b):
             rows = slice(b * P, (b + 1) * P)
@@ -125,7 +128,7 @@ def tile_graphlearner_s_kernel(tc, features, weight_tensor, out):
 
         def threshold(acc, width):
             sim = results.tile([P, WIDE], F32, name="sim")
-            nc.scalar.copy(out=sim[:, :width], in_=acc)
+            nc.scalar.copy(out=sim[:, :width], in_=acc[:, :width])
             adj = results.tile([P, WIDE], F32, name="adj")
             nc.vector.scalar_tensor_tensor(
                 out=adj[:, :width],
@@ -137,34 +140,44 @@ def tile_graphlearner_s_kernel(tc, features, weight_tensor, out):
             )
             return adj
 
-        for b in range(LEAD):
-            weigh(b)
-        for step in range(BLOCKS + 2):
-            if step < BLOCKS:
-                normalise(step)
-            if 0 <= step - 1 < BLOCKS:
-                pack(step - 1)
-            if step + LEAD < BLOCKS:
-                weigh(step + LEAD)
-            if 0 <= step - 2 < BLOCKS:
-                quantise(step - 2)
+        def finish_row(i):
+            left = 0
+            while left <= i:
+                count = {1: 1, 2: 2, 3: 3, 4: 4, 5: 4}[i + 1 - left]
+                acc = psum_s.tile([P, WIDE], F32, name="acc")
+                done = 0
+                while done < count:
+                    n = 4 if count - done >= 4 else (2 if count - done >= 2 else 1)
+                    similarity(acc[:, done * P : (done + n) * P], i, slice((left + done) * P, (left + done + n) * P))
+                    done += n
+                adj = threshold(acc, count * P)
+                nc.sync.dma_start(out=out[i * P : (i + 1) * P, left * P : (left + count) * P], in_=adj[:, : count * P])
+                left += count
 
-        for i in range(BLOCKS):
+        def finish_column(j):
             acc = psum_s.tile([P, WIDE], F32, name="acc")
-            similarity(acc[:], i, slice(0, WIDE))
-            adj = threshold(acc[:], WIDE)
-            nc.sync.dma_start(out=out[i * P : (i + 1) * P, 0:WIDE], in_=adj[:])
+            for i in range(j):
+                similarity(acc[:, i * P : (i + 1) * P], i, slice(j * P, (j + 1) * P))
+            adj = threshold(acc, j * P)
+            nc.sync.dma_start(
+                out=out[0 : j * P, j * P : (j + 1) * P].rearrange("(i p) m -> p i m", p=P),
+                in_=adj[:, : j * P].rearrange("p (i m) -> p i m", m=P),
+            )
 
-        last_cols = slice(WIDE, N_ROWS)
-        acc = psum_s.tile([P, WIDE], F32, name="acc")
-        for i in range(WIDE_BLOCKS):
-            similarity(acc[:, i * P : (i + 1) * P], i, last_cols)
-        adj = threshold(acc[:], WIDE)
-        nc.sync.dma_start(
-            out=out[0:WIDE, last_cols].rearrange("(i p) m -> p i m", p=P),
-            in_=adj[:].rearrange("p (i m) -> p i m", m=P),
-        )
-        acc = psum_s.tile([P, WIDE], F32, name="acc")
-        similarity(acc[:, 0:P], WIDE_BLOCKS, last_cols)
-        adj = threshold(acc[:, 0:P], P)
-        nc.sync.dma_start(out=out[WIDE:N_ROWS, last_cols], in_=adj[:, 0:P])
+        for b in range(BLOCKS):
+            weigh(b)
+        for b in range(BLOCKS + 1):
+            if b < BLOCKS:
+                sum_squares(b)
+            if b > 0:
+                root(b - 1)
+        for b in range(BLOCKS):
+            normalise(b)
+            transpose(b)
+        for b in range(BLOCKS):
+            pack(b)
+            quantise(b)
+        for b in range(BLOCKS):
+            finish_row(b)
+            if b > 0:
+                finish_column(b)

@@ -36,11 +36,11 @@ def tile_graphlearner_s_kernel(tc, features, weight_tensor, out):
         psum_s = ctx.enter_context(tc.psum_pool(name="psum_s", bufs=4))
         ctx.enter_context(tc.manual_schedule())
 
+        w_cols = consts.tile([P, PACK], BF16)
+        nc.sync.dma_start(out=w_cols[:], in_=weight_tensor.rearrange("o (p t) -> (o p) t", t=PACK))
         feat = keep.tile([P, BLOCKS, D], BF16)
         for b in range(BLOCKS):
             nc.sync.dma_start(out=feat[:, b, :], in_=features[b * P : (b + 1) * P, :])
-        w_cols = consts.tile([P, PACK], BF16)
-        nc.scalar.dma_start(out=w_cols[:], in_=weight_tensor.rearrange("o (p t) -> (o p) t", t=PACK))
 
         one_col = consts.tile([P, 1], F32)
         nc.vector.memset(one_col[:], 1.0)
@@ -89,9 +89,12 @@ def tile_graphlearner_s_kernel(tc, features, weight_tensor, out):
             col = slice(b, b + 1)
             nc.scalar.activation(out=rsqrt[:, col], in_=sumsq[:, col], func=ACT.Abs_reciprocal_sqrt)
 
-        def normalise(b):
+        def clamp(b):
             col = slice(b, b + 1)
             nc.vector.tensor_scalar_min(out=rnorm[:, col], in0=rsqrt[:, col], scalar1=1.0 / EPS)
+
+        def normalise(b):
+            col = slice(b, b + 1)
             c_b = work.tile([P, D], BF16, name="c_b")
             nc.vector.tensor_scalar_mul(out=c_b[:], in0=context[b][:], scalar1=rnorm[:, col])
             normalised[b] = c_b
@@ -171,7 +174,10 @@ def tile_graphlearner_s_kernel(tc, features, weight_tensor, out):
                 sum_squares(b)
             if b > 0:
                 root(b - 1)
+        clamp(0)
         for b in range(BLOCKS):
+            if b + 1 < BLOCKS:
+                clamp(b + 1)
             normalise(b)
             transpose(b)
         for b in range(BLOCKS):

@@ -36,10 +36,12 @@ def tile_graphlearner_s_kernel(tc, features, weight_tensor, out):
         psum_s = ctx.enter_context(tc.psum_pool(name="psum_s", bufs=4))
         ctx.enter_context(tc.manual_schedule())
 
-        w_cols = consts.tile([P, PACK], BF16)
-        nc.sync.dma_start(out=w_cols[:], in_=weight_tensor.rearrange("o (p t) -> (o p) t", t=PACK))
+        w_rows = consts.tile([P, P], BF16)
+        nc.vector.memset(w_rows[:].bitcast(U32), 0)
         feat = keep.tile([P, BLOCKS, D], BF16)
         for b in range(BLOCKS):
+            if b == 1:
+                nc.sync.dma_start(out=w_rows[0:PACK, :], in_=weight_tensor.rearrange("o (t p) -> (o t) p", p=P))
             nc.sync.dma_start(out=feat[:, b, :], in_=features[b * P : (b + 1) * P, :])
 
         one_col = consts.tile([P, 1], F32)
@@ -51,12 +53,12 @@ def tile_graphlearner_s_kernel(tc, features, weight_tensor, out):
         table_warm = consts.tile([P, 1], F32)
         nc.scalar.activation(out=table_warm[:], in_=one_col[:], func=ACT.Abs_reciprocal_sqrt)
 
-        w_all = psum_w.tile([P, PACK, P], F32)
+        w_all = psum_w.tile([P, D], F32)
         for t in range(PACK):
             nc.tensor.matmul(
-                out=w_all[:, t, :],
-                lhsT=w_cols[:, t : t + 1].to_broadcast([P, P]),
-                rhs=ident[:],
+                out=w_all[:, t * P : (t + 1) * P],
+                lhsT=ident[:, t : t + 1].to_broadcast([P, P]),
+                rhs=w_rows[:],
                 start=True,
                 stop=True,
             )
@@ -76,7 +78,7 @@ def tile_graphlearner_s_kernel(tc, features, weight_tensor, out):
             nc.vector.tensor_tensor(
                 out=ctx_b[:].rearrange("p (u n e) -> p u n e", u=2, e=2),
                 in0=feat[:, b, :].rearrange("p (n u e) -> p u n e", u=2, e=2),
-                in1=w_all[:].rearrange("p (u e) n -> p u n e", u=2),
+                in1=w_all[:].rearrange("p (n u e) -> p u n e", u=2, e=2),
                 op=ALU.mult,
             )
             context[b] = ctx_b

@@ -186,6 +186,6 @@ def tile_graphlearner_s_kernel(tc, features, weight_tensor, out):
             pack(b)
             quantise(b)
         for b in range(BLOCKS):
-            finish_row(b)
             if b > 0:
                 finish_column(b)
+            finish_row(b)

from contextlib import ExitStack

import concourse.mybir as mybir
from concourse.masks import make_identity

F32 = mybir.dt.float32
BF16 = mybir.dt.bfloat16
U32 = mybir.dt.uint32
U8 = mybir.dt.uint8
FP8X4 = mybir.dt.float8_e4m3fn_x4
ALU = mybir.AluOpType
ACT = mybir.ActivationFunctionType

P = 128
PACK = 4
N_ROWS = 640
D = 512
BLOCKS = N_ROWS // P
WIDE_BLOCKS = 4
WIDE = WIDE_BLOCKS * P
EPS = 1e-12
EPSILON = 0.65

FLOPS = 2 * N_ROWS * N_ROWS * D


def tile_graphlearner_s_kernel(tc, features, weight_tensor, out):
    nc = tc.nc
    with ExitStack() as ctx:
        consts = ctx.enter_context(tc.tile_pool(name="consts", bufs=1))
        keep = ctx.enter_context(tc.tile_pool(name="keep", bufs=1))
        work = ctx.enter_context(tc.tile_pool(name="work", bufs=BLOCKS))
        results = ctx.enter_context(tc.tile_pool(name="results", bufs=2 * BLOCKS))
        psum_w = ctx.enter_context(tc.psum_pool(name="psum_w", bufs=1))
        psum_t = ctx.enter_context(tc.psum_pool(name="psum_t", bufs=3))
        psum_s = ctx.enter_context(tc.psum_pool(name="psum_s", bufs=4))
        ctx.enter_context(tc.manual_schedule())

        w_rows = consts.tile([P, P], BF16)
        nc.vector.memset(w_rows[:].bitcast(U32), 0)
        feat = keep.tile([P, BLOCKS, D], BF16)
        for b in range(BLOCKS):
            if b == 1:
                nc.sync.dma_start(out=w_rows[0:PACK, :], in_=weight_tensor.rearrange("o (t p) -> (o t) p", p=P))
            nc.sync.dma_start(out=feat[:, b, :], in_=features[b * P : (b + 1) * P, :])

        one_col = consts.tile([P, 1], F32)
        nc.vector.memset(one_col[:], 1.0)
        ident = consts.tile([P, P], BF16)
        make_identity(nc, ident[:])
        ident_f32 = consts.tile([P, P], F32)
        make_identity(nc, ident_f32[:])
        table_warm = consts.tile([P, 1], F32)
        nc.scalar.activation(out=table_warm[:], in_=one_col[:], func=ACT.Abs_reciprocal_sqrt)

        w_all = psum_w.tile([P, D], F32)
        for t in range(PACK):
            nc.tensor.matmul(
                out=w_all[:, t * P : (t + 1) * P],
                lhsT=ident[:, t : t + 1].to_broadcast([P, P]),
                rhs=w_rows[:],
                start=True,
                stop=True,
            )

        sumsq = keep.tile([P, BLOCKS], F32)
        rsqrt = keep.tile([P, BLOCKS], F32)
        rnorm = keep.tile([P, BLOCKS], F32)
        grouped = keep.tile([P, BLOCKS, P, PACK], BF16, align_bytes=64)
        codes = keep.tile([P, N_ROWS], U32, align_bytes=64)
        scales = keep.tile([P, N_ROWS], U8, align_bytes=64)
        context = {}
        normalised = {}
        transposed = {}

        def weigh(b):
            ctx_b = work.tile([P, D], F32, name="ctx_b")
            nc.vector.tensor_tensor(
                out=ctx_b[:].rearrange("p (u n e) -> p u n e", u=2, e=2),
                in0=feat[:, b, :].rearrange("p (n u e) -> p u n e", u=2, e=2),
                in1=w_all[:].rearrange("p (n u e) -> p u n e", u=2, e=2),
                op=ALU.mult,
            )
            context[b] = ctx_b

        def sum_squares(b):
            squares = work.tile([P, D], BF16, name="squares")
            nc.scalar.activation(out=squares[:], in_=context[b][:], func=ACT.Square, accum_out=sumsq[:, b : b + 1])

        def root(b):
            col = slice(b, b + 1)
            nc.scalar.activation(out=rsqrt[:, col], in_=sumsq[:, col], func=ACT.Abs_reciprocal_sqrt)

        def clamp(b):
            col = slice(b, b + 1)
            nc.vector.tensor_scalar_min(out=rnorm[:, col], in0=rsqrt[:, col], scalar1=1.0 / EPS)

        def normalise(b):
            col = slice(b, b + 1)
            c_b = work.tile([P, D], BF16, name="c_b")
            nc.vector.tensor_scalar_mul(out=c_b[:], in0=context[b][:], scalar1=rnorm[:, col])
            normalised[b] = c_b

        def transpose(b):
            words = normalised[b][:].bitcast(F32)
            c_t = psum_t.tile([P, 2, P], F32, name="c_t")
            for u in range(2):
                nc.tensor.transpose(c_t[:, u, :], words[:, u * P : (u + 1) * P], ident_f32[:])
            transposed[b] = c_t

        def pack(b):
            nc.scalar.copy(out=grouped[:, b].bitcast(F32), in_=transposed[b][:].rearrange("p u r -> p r u"))

        def quantise(b):
            rows = slice(b * P, (b + 1) * P)
            nc.vector.quantize_mx(
                out=codes[:, rows].bitcast(FP8X4),
                scales=scales[:, rows],
                in_=grouped[:, b].rearrange("p r t -> p (r t)"),
            )

        def similarity(acc, i, cols):
            rows = slice(i * P, (i + 1) * P)
            nc.tensor.matmul_mx(
                out=acc,
                lhsT=codes[:, rows].bitcast(FP8X4),
                lhsT_scale=scales[:, rows],
                rhs=codes[:, cols].bitcast(FP8X4),
                rhs_scale=scales[:, cols],
                start=True,
                stop=True,
            )

        def threshold(acc, width):
            sim = results.tile([P, WIDE], F32, name="sim")
            nc.scalar.copy(out=sim[:, :width], in_=acc[:, :width])
            adj = results.tile([P, WIDE], F32, name="adj")
            nc.vector.scalar_tensor_tensor(
                out=adj[:, :width],
                in0=sim[:, :width],
                scalar=EPSILON,
                in1=sim[:, :width],
                op0=ALU.is_gt,
                op1=ALU.mult,
            )
            return adj

        def finish_row(i):
            left = 0
            while left <= i:
                count = {1: 1, 2: 2, 3: 3, 4: 4, 5: 4}[i + 1 - left]
                acc = psum_s.tile([P, WIDE], F32, name="acc")
                done = 0
                while done < count:
                    n = 4 if count - done >= 4 else (2 if count - done >= 2 else 1)
                    similarity(acc[:, done * P : (done + n) * P], i, slice((left + done) * P, (left + done + n) * P))
                    done += n
                adj = threshold(acc, count * P)
                nc.sync.dma_start(out=out[i * P : (i + 1) * P, left * P : (left + count) * P], in_=adj[:, : count * P])
                left += count

        def finish_column(j):
            acc = psum_s.tile([P, WIDE], F32, name="acc")
            for i in range(j):
                similarity(acc[:, i * P : (i + 1) * P], i, slice(j * P, (j + 1) * P))
            adj = threshold(acc, j * P)
            nc.sync.dma_start(
                out=out[0 : j * P, j * P : (j + 1) * P].rearrange("(i p) m -> p i m", p=P),
                in_=adj[:, : j * P].rearrange("p (i m) -> p i m", m=P),
            )

        for b in range(BLOCKS):
            weigh(b)
        for b in range(BLOCKS + 1):
            if b < BLOCKS:
                sum_squares(b)
            if b > 0:
                root(b - 1)
        clamp(0)
        for b in range(BLOCKS):
            if b + 1 < BLOCKS:
                clamp(b + 1)
            normalise(b)
            transpose(b)
        for b in range(BLOCKS):
            pack(b)
            quantise(b)
        for b in range(BLOCKS):
            if b > 0:
                finish_column(b)
            finish_row(b)
